import numpy as np
import ml_dtypes


def mxq(x, axis, fmt="e4m3"):
    dtype, down = {"e4m3": (ml_dtypes.float8_e4m3fn, 7), "e5m2": (ml_dtypes.float8_e5m2, 14)}[fmt]
    v = np.moveaxis(np.asarray(x, np.float32).astype(ml_dtypes.bfloat16).astype(np.float64), axis, -1)
    blocks = v.reshape(v.shape[:-1] + (-1, 32))
    amax = np.abs(blocks).max(-1, keepdims=True)
    byte = np.maximum(np.where(amax > 0, np.frexp(amax)[1] - 1 + 127, 0) - down, 1)
    scale = np.exp2(byte - 127.0)
    codes = (blocks / scale).astype(np.float32).astype(dtype).astype(np.float64)
    return np.moveaxis((codes * scale).reshape(v.shape), -1, axis)


WIDE = False


def mx_kscale(k):
    if not WIDE:
        return np.ones(k)
    levels = np.array([10, -10, 5, -5, 0])
    if k % 512:
        return np.exp2(np.random.permutation(np.resize(levels, k // 32))).repeat(32)
    a = np.empty((k // 512, 16))
    for p in range(k // 512):
        a[p, :8] = np.random.permutation(np.resize(levels, 8))
        for g in range(8):
            far = levels[np.abs(levels - a[p, g]) >= 10]
            a[p, g + 8] = far[np.random.randint(len(far))]
    return np.exp2(a.ravel()).repeat(32)


BF16 = ml_dtypes.bfloat16


def bf(x):
    return np.asarray(x, np.float32).astype(BF16)


def f64(x):
    return np.asarray(x).astype(np.float64)


B, C, H, W = 1, 2048, 32, 64
CK, CV = C // 8, C // 2
HP, WP = H // 2, W // 2
N, M = H * W, HP * WP


def maxpool2x2(v):
    return v.reshape(v.shape[0], v.shape[1], HP, 2, WP, 2).max(axis=(3, 5))


def setup_inputs():
    s = mx_kscale(C)
    a = 1.7 / CK ** 0.25
    return {"x": bf(np.random.standard_normal((B, C, H, W)) * s[:, None, None]),
            "w_phi": bf(np.random.standard_normal((CK, C)) * a / np.sqrt(C) / s),
            "w_g": bf(np.random.standard_normal((CV, C)) / np.sqrt(C) / s)}


def reference(x, w_phi, w_g):
    xq = mxq(f64(x).reshape(B, C, N), 1, "e4m3")
    u_phi = (mxq(f64(w_phi), 1, "e4m3") @ xq).reshape(B, CK, H, W)
    u_g = (mxq(f64(w_g), 1, "e4m3") @ xq).reshape(B, CV, H, W)
    phi = maxpool2x2(u_phi).reshape(B, CK, M)
    g = maxpool2x2(u_g).reshape(B, CV, M)
    return phi, g

@@ -1,0 +1,234 @@
+from contextlib import ExitStack
+
+import concourse.mybir as mybir
+from concourse.masks import make_identity
+
+BF16 = mybir.dt.bfloat16
+F32 = mybir.dt.float32
+U32 = mybir.dt.uint32
+U8 = mybir.dt.uint8
+FP8X4 = mybir.dt.float8_e4m3fn_x4
+
+P = 128
+PACK = 4
+K_PASS = P * PACK
+C = 2048
+PASSES = C // K_PASS
+HEIGHT, WIDTH = 32, 64
+PIXELS = HEIGHT * WIDTH
+N_BLOCK = 512
+N_BLOCKS = PIXELS // N_BLOCK
+POOLED_ROWS = N_BLOCK // WIDTH // 2
+POOLED_WIDTH = WIDTH // 2
+POOLED_BLOCK = POOLED_ROWS * POOLED_WIDTH
+PHI_TILES = 256 // P
+G_TILES = 1024 // P
+M_TILES = PHI_TILES + G_TILES
+WORDS = P
+WORD_BLOCKS = C // 2 // WORDS
+BANK_BLOCKS = 4
+OPEN_TILES = 6
+assert M_TILES - OPEN_TILES == PASSES
+RUN = 4
+SHARED_BLOCKS = 2
+POOL_LAG = 5
+BANKS = 8
+TURN_BANKS = 4
+TILES = M_TILES * N_BLOCKS
+
+FLOPS = 2 * M_TILES * P * C * PIXELS
+
+
+def tile_attention_pa_kernel(tc, x, w_phi, w_g, out_0, out_1):
+    nc = tc.nc
+    x_rows = x.rearrange("b c h w -> (b c) (h w)")
+    phi_rows = out_0.rearrange("b o m -> (b o) m")
+    g_rows = out_1.rearrange("b o m -> (b o) m")
+
+    def weight_rows(m):
+        if m < PHI_TILES:
+            return w_phi[m * P : (m + 1) * P, :]
+        return w_g[(m - PHI_TILES) * P : (m - PHI_TILES + 1) * P, :]
+
+    def output_rows(m):
+        if m < PHI_TILES:
+            return phi_rows[m * P : (m + 1) * P, :]
+        return g_rows[(m - PHI_TILES) * P : (m - PHI_TILES + 1) * P, :]
+
+    with ExitStack() as ctx:
+        keep = ctx.enter_context(tc.tile_pool(name="keep", bufs=1))
+        w_stage = ctx.enter_context(tc.tile_pool(name="w_stage", bufs=3))
+        x_stage = ctx.enter_context(tc.tile_pool(name="x_stage", bufs=3))
+        ctx.enter_context(tc.manual_schedule())
+
+        identity = keep.tile([P, P], F32, name="identity")
+        make_identity(nc, identity[:])
+
+        w_raw = [keep.tile([P, C], BF16, name="w_raw%d" % m) for m in range(M_TILES)]
+        w_codes = [
+            keep.tile([P, PASSES * P], U32, name="w_codes%d" % m, align_bytes=64)
+            for m in range(M_TILES)
+        ]
+        w_scales = [
+            keep.tile([P, PASSES * P], U8, name="w_scales%d" % m, align_bytes=64)
+            for m in range(M_TILES)
+        ]
+        x_raw = [
+            [keep.tile([P, PACK, N_BLOCK], BF16, name="x_raw%d_%d" % (b, g)) for g in range(PASSES)]
+            for b in range(N_BLOCKS)
+        ]
+        x_codes = [
+            [
+                keep.tile([P, N_BLOCK], U32, name="x_codes%d_%d" % (b, g), align_bytes=64)
+                for g in range(PASSES)
+            ]
+            for b in range(N_BLOCKS)
+        ]
+        x_scales = [
+            [
+                keep.tile([P, N_BLOCK], U8, name="x_scales%d_%d" % (b, g), align_bytes=64)
+                for g in range(PASSES)
+            ]
+            for b in range(N_BLOCKS)
+        ]
+        w_grouped = {}
+        x_grouped = {}
+        open_sums = {}
+        pooled_tiles = []
+
+        def load_weights(m):
+            nc.sync.dma_start(out=w_raw[m][:], in_=weight_rows(m))
+
+        def load_x(b, g):
+            nc.sync.dma_start(
+                out=x_raw[b][g][:],
+                in_=x_rows[
+                    g * K_PASS : (g + 1) * K_PASS, b * N_BLOCK : (b + 1) * N_BLOCK
+                ].rearrange("(p t) n -> p t n", t=PACK),
+            )
+
+        def flip_weights(turned, m):
+            grouped = w_stage.tile([P, C], BF16, name="w_grouped", tag="w_grouped", align_bytes=64)
+            grouped_words = grouped[:].bitcast(F32).rearrange(
+                "p (g o u) -> p g o u", g=PASSES, o=P, u=2
+            )
+            raw_words = w_raw[m][:].bitcast(F32)
+            passes_in_bank = BANK_BLOCKS // 2
+            for bank in range(WORD_BLOCKS // BANK_BLOCKS):
+                flipped = turned.tile([P, BANK_BLOCKS, P], F32, name="flipped", tag="flipped")
+                for q in range(BANK_BLOCKS):
+                    g, u = divmod(bank * BANK_BLOCKS + q, 2)
+                    nc.tensor.transpose(
+                        flipped[:, q, :],
+                        raw_words[:, 2 * g * WORDS + u : 2 * (g + 1) * WORDS : 2],
+                        identity[:],
+                    )
+                nc.scalar.copy(
+                    out=grouped_words[:, bank * passes_in_bank : (bank + 1) * passes_in_bank],
+                    in_=flipped[:].rearrange("p (g u) o -> p g o u", u=2),
+                )
+            w_grouped[m] = grouped
+
+        def quantise_weights(m):
+            nc.vector.quantize_mx(
+                out=w_codes[m][:].bitcast(FP8X4), scales=w_scales[m][:], in_=w_grouped[m][:]
+            )
+
+        def regroup_x(b, g):
+            grouped = x_stage.tile(
+                [P, N_BLOCK, PACK], BF16, name="x_grouped", tag="x_grouped", align_bytes=64
+            )
+            target = grouped[:].rearrange("p (c r) t -> p c t r", r=RUN)
+            source = x_raw[b][g][:].rearrange("p t (c r) -> p c t r", r=RUN)
+            vector_runs = (N_BLOCK // RUN) >> (b + 1) if b < SHARED_BLOCKS else 0
+            if vector_runs > 0:
+                nc.vector.tensor_copy(out=target[:, :vector_runs], in_=source[:, :vector_runs])
+            nc.scalar.copy(out=target[:, vector_runs:], in_=source[:, vector_runs:])
+            x_grouped[(b, g)] = grouped
+
+        def quantise_x(b, g):
+            nc.vector.quantize_mx(
+                out=x_codes[b][g][:].bitcast(FP8X4),
+                scales=x_scales[b][g][:],
+                in_=x_grouped[(b, g)][:].rearrange("p n t -> p (n t)"),
+            )
+
+        def open_sum(sums, s):
+            open_sums[s] = sums.tile([P, N_BLOCK], F32, name="acc", tag="acc")
+
+        def multiply(s, g):
+            b, m = divmod(s, M_TILES)
+            nc.tensor.matmul_mx(
+                out=open_sums[s][:],
+                lhsT=w_codes[m][:, g * P : (g + 1) * P].bitcast(FP8X4),
+                lhsT_scale=w_scales[m][:, g * P : (g + 1) * P],
+                rhs=x_codes[b][g][:].bitcast(FP8X4),
+                rhs_scale=x_scales[b][g][:],
+                start=(g == 0),
+                stop=(g == PASSES - 1),
+            )
+
+        def pool_tiles_before(limit):
+            for s in range(len(pooled_tiles), limit):
+                b, m = divmod(s, M_TILES)
+                pooled = keep.tile([P, POOLED_ROWS, POOLED_WIDTH], F32, name="pooled%d" % s)
+                nc.vector.tensor_reduce(
+                    out=pooled[:],
+                    in_=open_sums[s][:].rearrange(
+                        "p (i a j b) -> p i j a b", i=POOLED_ROWS, a=2, j=POOLED_WIDTH, b=2
+                    ),
+                    axis=mybir.AxisListType.XY,
+                    op=mybir.AluOpType.max,
+                )
+                nc.sync.dma_start(
+                    out=output_rows(m)[:, b * POOLED_BLOCK : (b + 1) * POOLED_BLOCK],
+                    in_=pooled[:].rearrange("p i j -> p (i j)"),
+                )
+                pooled_tiles.append(s)
+
+        for m in range(M_TILES):
+            load_weights(m)
+        for b in range(N_BLOCKS):
+            for g in range(PASSES):
+                load_x(b, g)
+
+        with tc.psum_pool(name="turned", bufs=TURN_BANKS) as turned:
+            for m in range(M_TILES):
+                flip_weights(turned, m)
+                quantise_weights(m)
+
+        with tc.psum_pool(name="sums", bufs=BANKS, reuse_waits="tile") as sums:
+
+            def whole_tile(s):
+                pool_tiles_before(s - POOL_LAG)
+                open_sum(sums, s)
+                for g in range(PASSES):
+                    multiply(s, g)
+
+            for s in range(OPEN_TILES):
+                open_sum(sums, s)
+            regroup_x(0, 0)
+            for g in range(PASSES):
+                if g + 1 < PASSES:
+                    regroup_x(0, g + 1)
+                quantise_x(0, g)
+                for s in range(OPEN_TILES):
+                    multiply(s, g)
+
+            regroup_x(1, 0)
+            for s in range(OPEN_TILES, M_TILES):
+                g = s - OPEN_TILES
+                if g + 1 < PASSES:
+                    regroup_x(1, g + 1)
+                quantise_x(1, g)
+                whole_tile(s)
+
+            for s in range(M_TILES, TILES):
+                b, m = divmod(s, M_TILES)
+                for g in range(PASSES):
+                    if b + 1 < N_BLOCKS and g * M_TILES // PASSES == m:
+                        regroup_x(b + 1, g)
+                    if b + 1 < N_BLOCKS and g * M_TILES // PASSES + 2 == m:
+                        quantise_x(b + 1, g)
+                whole_tile(s)
+            pool_tiles_before(TILES)

@@ -27,13 +27,14 @@ M_TILES = PHI_TILES + G_TILES
 WORDS = P
 WORD_BLOCKS = C // 2 // WORDS
 BANK_BLOCKS = 4
-OPEN_TILES = 6
-assert M_TILES - OPEN_TILES == PASSES
+FIRST_TILES = 6
 RUN = 4
-SHARED_BLOCKS = 2
-POOL_LAG = 5
+RUNS = N_BLOCK // RUN
+VECTOR_RUNS = [[RUNS, 3 * RUNS // 4, RUNS // 2, RUNS // 2], [RUNS // 4, RUNS // 2, RUNS // 2, RUNS // 2]]
+LATER_VECTOR_RUNS = RUNS // 4
+VECTOR_EMPTIES = (1, 3, 5)
+POOL_LAG = 4
 BANKS = 8
-TURN_BANKS = 4
 TILES = M_TILES * N_BLOCKS
 
 FLOPS = 2 * M_TILES * P * C * PIXELS
@@ -58,7 +59,8 @@ def tile_attention_pa_kernel(tc, x, w_phi, w_g, out_0, out_1):
     with ExitStack() as ctx:
         keep = ctx.enter_context(tc.tile_pool(name="keep", bufs=1))
         w_stage = ctx.enter_context(tc.tile_pool(name="w_stage", bufs=3))
-        x_stage = ctx.enter_context(tc.tile_pool(name="x_stage", bufs=3))
+        x_stage = ctx.enter_context(tc.tile_pool(name="x_stage", bufs=5))
+        psum = ctx.enter_context(tc.psum_pool(name="psum", bufs=1))
         ctx.enter_context(tc.manual_schedule())
 
         identity = keep.tile([P, P], F32, name="identity")
@@ -94,7 +96,7 @@ def tile_attention_pa_kernel(tc, x, w_phi, w_g, out_0, out_1):
         w_grouped = {}
         x_grouped = {}
         open_sums = {}
-        pooled_tiles = []
+        finished = []
 
         def load_weights(m):
             nc.sync.dma_start(out=w_raw[m][:], in_=weight_rows(m))
@@ -107,7 +109,10 @@ def tile_attention_pa_kernel(tc, x, w_phi, w_g, out_0, out_1):
                 ].rearrange("(p t) n -> p t n", t=PACK),
             )
 
-        def flip_weights(turned, m):
+        def shared_bank(i):
+            return "bank%d" % (i % BANKS)
+
+        def flip_weights(m):
             grouped = w_stage.tile([P, C], BF16, name="w_grouped", tag="w_grouped", align_bytes=64)
             grouped_words = grouped[:].bitcast(F32).rearrange(
                 "p (g o u) -> p g o u", g=PASSES, o=P, u=2
@@ -115,7 +120,10 @@ def tile_attention_pa_kernel(tc, x, w_phi, w_g, out_0, out_1):
             raw_words = w_raw[m][:].bitcast(F32)
             passes_in_bank = BANK_BLOCKS // 2
             for bank in range(WORD_BLOCKS // BANK_BLOCKS):
-                flipped = turned.tile([P, BANK_BLOCKS, P], F32, name="flipped", tag="flipped")
+                flipped = psum.tile(
+                    [P, BANK_BLOCKS, P], F32, name="flipped",
+                    tag=shared_bank(2 * m + bank),
+                )
                 for q in range(BANK_BLOCKS):
                     g, u = divmod(bank * BANK_BLOCKS + q, 2)
                     nc.tensor.transpose(
@@ -123,7 +131,10 @@ def tile_attention_pa_kernel(tc, x, w_phi, w_g, out_0, out_1):
                         raw_words[:, 2 * g * WORDS + u : 2 * (g + 1) * WORDS : 2],
                         identity[:],
                     )
-                nc.scalar.copy(
+                copy = nc.scalar.copy
+                if bank == 1 and m in VECTOR_EMPTIES:
+                    copy = nc.vector.tensor_copy
+                copy(
                     out=grouped_words[:, bank * passes_in_bank : (bank + 1) * passes_in_bank],
                     in_=flipped[:].rearrange("p (g u) o -> p g o u", u=2),
                 )
@@ -134,17 +145,28 @@ def tile_attention_pa_kernel(tc, x, w_phi, w_g, out_0, out_1):
                 out=w_codes[m][:].bitcast(FP8X4), scales=w_scales[m][:], in_=w_grouped[m][:]
             )
 
-        def regroup_x(b, g):
-            grouped = x_stage.tile(
-                [P, N_BLOCK, PACK], BF16, name="x_grouped", tag="x_grouped", align_bytes=64
-            )
-            target = grouped[:].rearrange("p (c r) t -> p c t r", r=RUN)
+        def regrouped(b, g):
+            if (b, g) not in x_grouped:
+                x_grouped[(b, g)] = x_stage.tile(
+                    [P, N_BLOCK, PACK], BF16, name="x_grouped", tag="x_grouped", align_bytes=64
+                )
+            target = x_grouped[(b, g)][:].rearrange("p (c r) t -> p c t r", r=RUN)
             source = x_raw[b][g][:].rearrange("p t (c r) -> p c t r", r=RUN)
-            vector_runs = (N_BLOCK // RUN) >> (b + 1) if b < SHARED_BLOCKS else 0
-            if vector_runs > 0:
-                nc.vector.tensor_copy(out=target[:, :vector_runs], in_=source[:, :vector_runs])
-            nc.scalar.copy(out=target[:, vector_runs:], in_=source[:, vector_runs:])
-            x_grouped[(b, g)] = grouped
+            return target, source
+
+        def vector_runs(b, g):
+            return VECTOR_RUNS[b][g] if b < len(VECTOR_RUNS) else LATER_VECTOR_RUNS
+
+        def regroup_on_vector(b, g):
+            target, source = regrouped(b, g)
+            share = slice(0, vector_runs(b, g))
+            nc.vector.tensor_copy(out=target[:, share], in_=source[:, share])
+
+        def regroup_on_scalar(b, g):
+            target, source = regrouped(b, g)
+            share = slice(vector_runs(b, g), RUNS)
+            if vector_runs(b, g) < RUNS:
+                nc.scalar.copy(out=target[:, share], in_=source[:, share])
 
         def quantise_x(b, g):
             nc.vector.quantize_mx(
@@ -153,11 +175,12 @@ def tile_attention_pa_kernel(tc, x, w_phi, w_g, out_0, out_1):
                 in_=x_grouped[(b, g)][:].rearrange("p n t -> p (n t)"),
             )
 
-        def open_sum(sums, s):
-            open_sums[s] = sums.tile([P, N_BLOCK], F32, name="acc", tag="acc")
-
         def multiply(s, g):
             b, m = divmod(s, M_TILES)
+            if g == 0:
+                open_sums[s] = psum.tile(
+                    [P, N_BLOCK], F32, name="acc", tag=shared_bank(2 * M_TILES + s)
+                )
             nc.tensor.matmul_mx(
                 out=open_sums[s][:],
                 lhsT=w_codes[m][:, g * P : (g + 1) * P].bitcast(FP8X4),
@@ -167,9 +190,13 @@ def tile_attention_pa_kernel(tc, x, w_phi, w_g, out_0, out_1):
                 start=(g == 0),
                 stop=(g == PASSES - 1),
             )
+            if g == PASSES - 1:
+                finished.append(s)
 
-        def pool_tiles_before(limit):
-            for s in range(len(pooled_tiles), limit):
+        def pool_tiles(keep_back):
+            while len(finished) > keep_back:
+                s = finished[0]
+                finished.remove(s)
                 b, m = divmod(s, M_TILES)
                 pooled = keep.tile([P, POOLED_ROWS, POOLED_WIDTH], F32, name="pooled%d" % s)
                 nc.vector.tensor_reduce(
@@ -184,51 +211,58 @@ def tile_attention_pa_kernel(tc, x, w_phi, w_g, out_0, out_1):
                     out=output_rows(m)[:, b * POOLED_BLOCK : (b + 1) * POOLED_BLOCK],
                     in_=pooled[:].rearrange("p i j -> p (i j)"),
                 )
-                pooled_tiles.append(s)
 
-        for m in range(M_TILES):
+        def regroup_x(b, g):
+            regroup_on_vector(b, g)
+            regroup_on_scalar(b, g)
+
+        for m in range(M_TILES - 1):
             load_weights(m)
+        load_x(0, 0)
+        load_weights(M_TILES - 1)
         for b in range(N_BLOCKS):
             for g in range(PASSES):
-                load_x(b, g)
+                if (b, g) != (0, 0):
+                    load_x(b, g)
 
-        with tc.psum_pool(name="turned", bufs=TURN_BANKS) as turned:
-            for m in range(M_TILES):
-                flip_weights(turned, m)
-                quantise_weights(m)
+        for m in range(M_TILES - 1):
+            flip_weights(m)
+            if 0 < m < M_TILES - 2:
+                quantise_weights(m - 1)
+        regroup_x(0, 0)
+        quantise_weights(M_TILES - 3)
+        quantise_x(0, 0)
+        flip_weights(M_TILES - 1)
+        regroup_x(0, 1)
+        quantise_weights(M_TILES - 2)
+        quantise_x(0, 1)
+        quantise_weights(M_TILES - 1)
 
-        with tc.psum_pool(name="sums", bufs=BANKS, reuse_waits="tile") as sums:
+        passes = [(b, g) for b in range(2) for g in range(PASSES)]
+        for g in range(PASSES):
+            for s in range(FIRST_TILES):
+                multiply(s, g)
+            if 0 < g < PASSES - 1:
+                quantise_x(0, g + 1)
+            regroup_x(*passes[g + 2])
 
-            def whole_tile(s):
-                pool_tiles_before(s - POOL_LAG)
-                open_sum(sums, s)
-                for g in range(PASSES):
-                    multiply(s, g)
+        for s in range(FIRST_TILES, M_TILES):
+            g = s - FIRST_TILES
+            quantise_x(1, g)
+            if g + 2 < PASSES:
+                regroup_x(1, g + 2)
+            pool_tiles(POOL_LAG)
+            for i in range(PASSES):
+                multiply(s, i)
 
-            for s in range(OPEN_TILES):
-                open_sum(sums, s)
-            regroup_x(0, 0)
+        for s in range(M_TILES, TILES):
+            b, m = divmod(s, M_TILES)
             for g in range(PASSES):
-                if g + 1 < PASSES:
-                    regroup_x(0, g + 1)
-                quantise_x(0, g)
-                for s in range(OPEN_TILES):
-                    multiply(s, g)
-
-            regroup_x(1, 0)
-            for s in range(OPEN_TILES, M_TILES):
-                g = s - OPEN_TILES
-                if g + 1 < PASSES:
-                    regroup_x(1, g + 1)
-                quantise_x(1, g)
-                whole_tile(s)
-
-            for s in range(M_TILES, TILES):
-                b, m = divmod(s, M_TILES)
-                for g in range(PASSES):
-                    if b + 1 < N_BLOCKS and g * M_TILES // PASSES == m:
-                        regroup_x(b + 1, g)
-                    if b + 1 < N_BLOCKS and g * M_TILES // PASSES + 2 == m:
-                        quantise_x(b + 1, g)
-                whole_tile(s)
-            pool_tiles_before(TILES)
+                if b + 1 < N_BLOCKS and g * M_TILES // PASSES == m:
+                    regroup_x(b + 1, g)
+                if b + 1 < N_BLOCKS and g * M_TILES // PASSES + 2 == m:
+                    quantise_x(b + 1, g)
+            pool_tiles(POOL_LAG)
+            for g in range(PASSES):
+                multiply(s, g)
+        pool_tiles(0)

@@ -27,11 +27,12 @@ M_TILES = PHI_TILES + G_TILES
 WORDS = P
 WORD_BLOCKS = C // 2 // WORDS
 BANK_BLOCKS = 4
+EARLY_TILES = 8
 FIRST_TILES = 6
 RUN = 4
 RUNS = N_BLOCK // RUN
-VECTOR_RUNS = [[RUNS, 3 * RUNS // 4, RUNS // 2, RUNS // 2], [RUNS // 4, RUNS // 2, RUNS // 2, RUNS // 2]]
-LATER_VECTOR_RUNS = RUNS // 4
+VECTOR_RUNS = [[96, 64, 64, 64], [32, 48, 48, 48]]
+LATER_VECTOR_RUNS = 16
 VECTOR_EMPTIES = (1, 3, 5)
 POOL_LAG = 4
 BANKS = 8
@@ -175,40 +176,47 @@ def tile_attention_pa_kernel(tc, x, w_phi, w_g, out_0, out_1):
                 in_=x_grouped[(b, g)][:].rearrange("p n t -> p (n t)"),
             )
 
-        def multiply(s, g):
+        def multiply(s, g, part=0, parts=1):
             b, m = divmod(s, M_TILES)
+            width = N_BLOCK // parts
+            pixels = slice(part * width, (part + 1) * width)
             if g == 0:
-                open_sums[s] = psum.tile(
-                    [P, N_BLOCK], F32, name="acc", tag=shared_bank(2 * M_TILES + s)
+                open_sums[(s, part)] = psum.tile(
+                    [P, width], F32, name="acc", tag=shared_bank(2 * M_TILES + s + part)
                 )
             nc.tensor.matmul_mx(
-                out=open_sums[s][:],
+                out=open_sums[(s, part)][:],
                 lhsT=w_codes[m][:, g * P : (g + 1) * P].bitcast(FP8X4),
                 lhsT_scale=w_scales[m][:, g * P : (g + 1) * P],
-                rhs=x_codes[b][g][:].bitcast(FP8X4),
-                rhs_scale=x_scales[b][g][:],
+                rhs=x_codes[b][g][:, pixels].bitcast(FP8X4),
+                rhs_scale=x_scales[b][g][:, pixels],
                 start=(g == 0),
                 stop=(g == PASSES - 1),
             )
             if g == PASSES - 1:
-                finished.append(s)
+                finished.append((s, part, parts))
 
         def pool_tiles(keep_back):
             while len(finished) > keep_back:
-                s = finished[0]
-                finished.remove(s)
+                s, part, parts = finished[0]
+                finished.remove(finished[0])
                 b, m = divmod(s, M_TILES)
-                pooled = keep.tile([P, POOLED_ROWS, POOLED_WIDTH], F32, name="pooled%d" % s)
+                pooled = keep.tile(
+                    [P, POOLED_ROWS // parts, POOLED_WIDTH], F32, name="pooled%d_%d" % (s, part)
+                )
                 nc.vector.tensor_reduce(
                     out=pooled[:],
-                    in_=open_sums[s][:].rearrange(
-                        "p (i a j b) -> p i j a b", i=POOLED_ROWS, a=2, j=POOLED_WIDTH, b=2
+                    in_=open_sums[(s, part)][:].rearrange(
+                        "p (i a j b) -> p i j a b",
+                        i=POOLED_ROWS // parts, a=2, j=POOLED_WIDTH, b=2,
                     ),
                     axis=mybir.AxisListType.XY,
                     op=mybir.AluOpType.max,
                 )
+                width = POOLED_BLOCK // parts
+                first = b * POOLED_BLOCK + part * width
                 nc.sync.dma_start(
-                    out=output_rows(m)[:, b * POOLED_BLOCK : (b + 1) * POOLED_BLOCK],
+                    out=output_rows(m)[:, first : first + width],
                     in_=pooled[:].rearrange("p i j -> p (i j)"),
                 )
 
@@ -216,27 +224,29 @@ def tile_attention_pa_kernel(tc, x, w_phi, w_g, out_0, out_1):
             regroup_on_vector(b, g)
             regroup_on_scalar(b, g)
 
-        for m in range(M_TILES - 1):
+        for m in range(EARLY_TILES):
             load_weights(m)
         load_x(0, 0)
-        load_weights(M_TILES - 1)
+        for m in range(EARLY_TILES, M_TILES):
+            load_weights(m)
         for b in range(N_BLOCKS):
             for g in range(PASSES):
                 if (b, g) != (0, 0):
                     load_x(b, g)
 
-        for m in range(M_TILES - 1):
+        for m in range(EARLY_TILES):
             flip_weights(m)
-            if 0 < m < M_TILES - 2:
+            if m > 0:
                 quantise_weights(m - 1)
         regroup_x(0, 0)
-        quantise_weights(M_TILES - 3)
+        flip_weights(8)
+        quantise_weights(7)
         quantise_x(0, 0)
-        flip_weights(M_TILES - 1)
+        flip_weights(9)
+        quantise_weights(8)
         regroup_x(0, 1)
-        quantise_weights(M_TILES - 2)
+        quantise_weights(9)
         quantise_x(0, 1)
-        quantise_weights(M_TILES - 1)
 
         passes = [(b, g) for b in range(2) for g in range(PASSES)]
         for g in range(PASSES):
@@ -255,7 +265,7 @@ def tile_attention_pa_kernel(tc, x, w_phi, w_g, out_0, out_1):
             for i in range(PASSES):
                 multiply(s, i)
 
-        for s in range(M_TILES, TILES):
+        for s in range(M_TILES, TILES - 1):
             b, m = divmod(s, M_TILES)
             for g in range(PASSES):
                 if b + 1 < N_BLOCKS and g * M_TILES // PASSES == m:
@@ -265,4 +275,9 @@ def tile_attention_pa_kernel(tc, x, w_phi, w_g, out_0, out_1):
             pool_tiles(POOL_LAG)
             for g in range(PASSES):
                 multiply(s, g)
+
+        for part in range(2):
+            pool_tiles(1)
+            for g in range(PASSES):
+                multiply(TILES - 1, g, part, 2)
         pool_tiles(0)

@@ -47,15 +47,9 @@ def tile_attention_pa_kernel(tc, x, w_phi, w_g, out_0, out_1):
     phi_rows = out_0.rearrange("b o m -> (b o) m")
     g_rows = out_1.rearrange("b o m -> (b o) m")
 
-    def weight_rows(m):
-        if m < PHI_TILES:
-            return w_phi[m * P : (m + 1) * P, :]
-        return w_g[(m - PHI_TILES) * P : (m - PHI_TILES + 1) * P, :]
-
-    def output_rows(m):
-        if m < PHI_TILES:
-            return phi_rows[m * P : (m + 1) * P, :]
-        return g_rows[(m - PHI_TILES) * P : (m - PHI_TILES + 1) * P, :]
+    def pair_rows(first, rest, pair):
+        rows = first if pair == 0 else rest[(pair - 1) * 2 * P : pair * 2 * P, :]
+        return rows.rearrange("(p j) c -> p j c", j=2)
 
     with ExitStack() as ctx:
         keep = ctx.enter_context(tc.tile_pool(name="keep", bufs=1))
@@ -67,7 +61,8 @@ def tile_attention_pa_kernel(tc, x, w_phi, w_g, out_0, out_1):
         identity = keep.tile([P, P], F32, name="identity")
         make_identity(nc, identity[:])
 
-        w_raw = [keep.tile([P, C], BF16, name="w_raw%d" % m) for m in range(M_TILES)]
+        w_pairs = [keep.tile([P, 2, C], BF16, name="w_raw%d" % i) for i in range(M_TILES // 2)]
+        w_raw = [w_pairs[m // 2][:, m % 2, :] for m in range(M_TILES)]
         w_codes = [
             keep.tile([P, PASSES * P], U32, name="w_codes%d" % m, align_bytes=64)
             for m in range(M_TILES)
@@ -99,8 +94,11 @@ def tile_attention_pa_kernel(tc, x, w_phi, w_g, out_0, out_1):
         open_sums = {}
         finished = []
 
+        def load_weight_pair(i):
+            nc.sync.dma_start(out=w_pairs[i][:], in_=pair_rows(w_phi, w_g, i))
+
         def load_weights(m):
-            nc.sync.dma_start(out=w_raw[m][:], in_=weight_rows(m))
+            nc.sync.dma_start(out=w_raw[m], in_=pair_rows(w_phi, w_g, m // 2)[:, m % 2, :])
 
         def load_x(b, g):
             nc.sync.dma_start(
@@ -118,7 +116,7 @@ def tile_attention_pa_kernel(tc, x, w_phi, w_g, out_0, out_1):
             grouped_words = grouped[:].bitcast(F32).rearrange(
                 "p (g o u) -> p g o u", g=PASSES, o=P, u=2
             )
-            raw_words = w_raw[m][:].bitcast(F32)
+            raw_words = w_raw[m].bitcast(F32)
             passes_in_bank = BANK_BLOCKS // 2
             for bank in range(WORD_BLOCKS // BANK_BLOCKS):
                 flipped = psum.tile(
@@ -216,7 +214,7 @@ def tile_attention_pa_kernel(tc, x, w_phi, w_g, out_0, out_1):
                 width = POOLED_BLOCK // parts
                 first = b * POOLED_BLOCK + part * width
                 nc.sync.dma_start(
-                    out=output_rows(m)[:, first : first + width],
+                    out=pair_rows(phi_rows, g_rows, m // 2)[:, m % 2, first : first + width],
                     in_=pooled[:].rearrange("p i j -> p (i j)"),
                 )
 
@@ -224,8 +222,10 @@ def tile_attention_pa_kernel(tc, x, w_phi, w_g, out_0, out_1):
             regroup_on_vector(b, g)
             regroup_on_scalar(b, g)
 
-        for m in range(EARLY_TILES):
-            load_weights(m)
+        load_weights(0)
+        load_weights(1)
+        for i in range(1, EARLY_TILES // 2):
+            load_weight_pair(i)
         load_x(0, 0)
         for m in range(EARLY_TILES, M_TILES):
             load_weights(m)

@@ -34,6 +34,7 @@ RUNS = N_BLOCK // RUN
 VECTOR_RUNS = [[96, 64, 64, 64], [32, 48, 48, 48]]
 LATER_VECTOR_RUNS = 16
 VECTOR_EMPTIES = (1, 3, 5)
+SCALE_ROW = 4
 POOL_LAG = 4
 BANKS = 8
 TILES = M_TILES * N_BLOCKS
@@ -141,7 +142,9 @@ def tile_attention_pa_kernel(tc, x, w_phi, w_g, out_0, out_1):
 
         def quantise_weights(m):
             nc.vector.quantize_mx(
-                out=w_codes[m][:].bitcast(FP8X4), scales=w_scales[m][:], in_=w_grouped[m][:]
+                out=w_codes[m][:].bitcast(FP8X4),
+                scales=w_scales[m][SCALE_ROW:, :],
+                in_=w_grouped[m][:],
             )
 
         def regrouped(b, g):
@@ -185,7 +188,7 @@ def tile_attention_pa_kernel(tc, x, w_phi, w_g, out_0, out_1):
             nc.tensor.matmul_mx(
                 out=open_sums[(s, part)][:],
                 lhsT=w_codes[m][:, g * P : (g + 1) * P].bitcast(FP8X4),
-                lhsT_scale=w_scales[m][:, g * P : (g + 1) * P],
+                lhsT_scale=w_scales[m][SCALE_ROW:, g * P : (g + 1) * P],
                 rhs=x_codes[b][g][:, pixels].bitcast(FP8X4),
                 rhs_scale=x_scales[b][g][:, pixels],
                 start=(g == 0),
@@ -222,9 +225,7 @@ def tile_attention_pa_kernel(tc, x, w_phi, w_g, out_0, out_1):
             regroup_on_vector(b, g)
             regroup_on_scalar(b, g)
 
-        load_weights(0)
-        load_weights(1)
-        for i in range(1, EARLY_TILES // 2):
+        for i in range(EARLY_TILES // 2):
             load_weight_pair(i)
         load_x(0, 0)
         for m in range(EARLY_TILES, M_TILES):
@@ -236,12 +237,13 @@ def tile_attention_pa_kernel(tc, x, w_phi, w_g, out_0, out_1):
 
         for m in range(EARLY_TILES):
             flip_weights(m)
-            if m > 0:
+            if 0 < m < EARLY_TILES - 1:
                 quantise_weights(m - 1)
         regroup_x(0, 0)
+        quantise_weights(6)
         flip_weights(8)
-        quantise_weights(7)
         quantise_x(0, 0)
+        quantise_weights(7)
         flip_weights(9)
         quantise_weights(8)
         regroup_x(0, 1)

@@ -28,13 +28,12 @@ WORDS = P
 WORD_BLOCKS = C // 2 // WORDS
 BANK_BLOCKS = 4
 EARLY_TILES = 8
-FIRST_TILES = 6
+FIRST_TILES = 8
+SECOND_TILES = 4
 RUN = 4
 RUNS = N_BLOCK // RUN
-VECTOR_RUNS = [[96, 64, 64, 64], [32, 48, 48, 48]]
-LATER_VECTOR_RUNS = 16
+VECTOR_RUNS = [[3 * RUNS // 4, 3 * RUNS // 4, RUNS // 2, RUNS // 2]] + [[RUNS // 8] * PASSES] * (N_BLOCKS - 1)
 VECTOR_EMPTIES = (1, 3, 5)
-SCALE_ROW = 4
 POOL_LAG = 4
 BANKS = 8
 TILES = M_TILES * N_BLOCKS
@@ -54,7 +53,7 @@ def tile_attention_pa_kernel(tc, x, w_phi, w_g, out_0, out_1):
 
     with ExitStack() as ctx:
         keep = ctx.enter_context(tc.tile_pool(name="keep", bufs=1))
-        w_stage = ctx.enter_context(tc.tile_pool(name="w_stage", bufs=3))
+        w_stage = ctx.enter_context(tc.tile_pool(name="w_stage", bufs=4))
         x_stage = ctx.enter_context(tc.tile_pool(name="x_stage", bufs=5))
         psum = ctx.enter_context(tc.psum_pool(name="psum", bufs=1))
         ctx.enter_context(tc.manual_schedule())
@@ -143,7 +142,7 @@ def tile_attention_pa_kernel(tc, x, w_phi, w_g, out_0, out_1):
         def quantise_weights(m):
             nc.vector.quantize_mx(
                 out=w_codes[m][:].bitcast(FP8X4),
-                scales=w_scales[m][SCALE_ROW:, :],
+                scales=w_scales[m][:],
                 in_=w_grouped[m][:],
             )
 
@@ -157,7 +156,7 @@ def tile_attention_pa_kernel(tc, x, w_phi, w_g, out_0, out_1):
             return target, source
 
         def vector_runs(b, g):
-            return VECTOR_RUNS[b][g] if b < len(VECTOR_RUNS) else LATER_VECTOR_RUNS
+            return VECTOR_RUNS[b][g]
 
         def regroup_on_vector(b, g):
             target, source = regrouped(b, g)
@@ -188,7 +187,7 @@ def tile_attention_pa_kernel(tc, x, w_phi, w_g, out_0, out_1):
             nc.tensor.matmul_mx(
                 out=open_sums[(s, part)][:],
                 lhsT=w_codes[m][:, g * P : (g + 1) * P].bitcast(FP8X4),
-                lhsT_scale=w_scales[m][SCALE_ROW:, g * P : (g + 1) * P],
+                lhsT_scale=w_scales[m][:, g * P : (g + 1) * P],
                 rhs=x_codes[b][g][:, pixels].bitcast(FP8X4),
                 rhs_scale=x_scales[b][g][:, pixels],
                 start=(g == 0),
@@ -245,10 +244,14 @@ def tile_attention_pa_kernel(tc, x, w_phi, w_g, out_0, out_1):
         quantise_x(0, 0)
         quantise_weights(7)
         flip_weights(9)
-        quantise_weights(8)
         regroup_x(0, 1)
-        quantise_weights(9)
+        quantise_weights(8)
         quantise_x(0, 1)
+        quantise_weights(9)
+
+        def whole_tile(s):
+            for g in range(PASSES):
+                multiply(s, g)
 
         passes = [(b, g) for b in range(2) for g in range(PASSES)]
         for g in range(PASSES):
@@ -256,27 +259,39 @@ def tile_attention_pa_kernel(tc, x, w_phi, w_g, out_0, out_1):
                 multiply(s, g)
             if 0 < g < PASSES - 1:
                 quantise_x(0, g + 1)
-            regroup_x(*passes[g + 2])
+            if g < PASSES - 1:
+                regroup_x(*passes[g + 2])
 
-        for s in range(FIRST_TILES, M_TILES):
-            g = s - FIRST_TILES
-            quantise_x(1, g)
+        pool_tiles(FIRST_TILES - 1)
+        regroup_x(1, 1)
+        pool_tiles(FIRST_TILES - 2)
+        quantise_x(1, 0)
+        pool_tiles(POOL_LAG + 1)
+        whole_tile(FIRST_TILES)
+        pool_tiles(POOL_LAG)
+        whole_tile(FIRST_TILES + 1)
+        regroup_x(1, 2)
+        quantise_x(1, 1)
+        pool_tiles(POOL_LAG)
+        for g in range(PASSES):
+            for m in range(SECOND_TILES):
+                multiply(M_TILES + m, g)
+            if g + 3 < PASSES:
+                regroup_x(1, g + 3)
             if g + 2 < PASSES:
-                regroup_x(1, g + 2)
-            pool_tiles(POOL_LAG)
-            for i in range(PASSES):
-                multiply(s, i)
+                quantise_x(1, g + 2)
 
-        for s in range(M_TILES, TILES - 1):
+        for s in range(M_TILES + SECOND_TILES, TILES - 1):
             b, m = divmod(s, M_TILES)
+            left = M_TILES - SECOND_TILES if b == 1 else M_TILES
             for g in range(PASSES):
-                if b + 1 < N_BLOCKS and g * M_TILES // PASSES == m:
+                beside = M_TILES - left + g * left // PASSES
+                if b + 1 < N_BLOCKS and beside == m:
                     regroup_x(b + 1, g)
-                if b + 1 < N_BLOCKS and g * M_TILES // PASSES + 2 == m:
+                if b + 1 < N_BLOCKS and min(beside + 2, M_TILES - 1) == m:
                     quantise_x(b + 1, g)
             pool_tiles(POOL_LAG)
-            for g in range(PASSES):
-                multiply(s, g)
+            whole_tile(s)
 
         for part in range(2):
             pool_tiles(1)

@@ -224,7 +224,9 @@ def tile_attention_pa_kernel(tc, x, w_phi, w_g, out_0, out_1):
             regroup_on_vector(b, g)
             regroup_on_scalar(b, g)
 
-        for i in range(EARLY_TILES // 2):
+        load_weights(0)
+        load_weights(1)
+        for i in range(1, EARLY_TILES // 2):
             load_weight_pair(i)
         load_x(0, 0)
         for m in range(EARLY_TILES, M_TILES):

from contextlib import ExitStack

import concourse.mybir as mybir
from concourse.masks import make_identity

BF16 = mybir.dt.bfloat16
F32 = mybir.dt.float32
U32 = mybir.dt.uint32
U8 = mybir.dt.uint8
FP8X4 = mybir.dt.float8_e4m3fn_x4

P = 128
PACK = 4
K_PASS = P * PACK
C = 2048
PASSES = C // K_PASS
HEIGHT, WIDTH = 32, 64
PIXELS = HEIGHT * WIDTH
N_BLOCK = 512
N_BLOCKS = PIXELS // N_BLOCK
POOLED_ROWS = N_BLOCK // WIDTH // 2
POOLED_WIDTH = WIDTH // 2
POOLED_BLOCK = POOLED_ROWS * POOLED_WIDTH
PHI_TILES = 256 // P
G_TILES = 1024 // P
M_TILES = PHI_TILES + G_TILES
WORDS = P
WORD_BLOCKS = C // 2 // WORDS
BANK_BLOCKS = 4
EARLY_TILES = 8
FIRST_TILES = 8
SECOND_TILES = 4
RUN = 4
RUNS = N_BLOCK // RUN
VECTOR_RUNS = [[3 * RUNS // 4, 3 * RUNS // 4, RUNS // 2, RUNS // 2]] + [[RUNS // 8] * PASSES] * (N_BLOCKS - 1)
VECTOR_EMPTIES = (1, 3, 5)
POOL_LAG = 4
BANKS = 8
TILES = M_TILES * N_BLOCKS

FLOPS = 2 * M_TILES * P * C * PIXELS


def tile_attention_pa_kernel(tc, x, w_phi, w_g, out_0, out_1):
    nc = tc.nc
    x_rows = x.rearrange("b c h w -> (b c) (h w)")
    phi_rows = out_0.rearrange("b o m -> (b o) m")
    g_rows = out_1.rearrange("b o m -> (b o) m")

    def pair_rows(first, rest, pair):
        rows = first if pair == 0 else rest[(pair - 1) * 2 * P : pair * 2 * P, :]
        return rows.rearrange("(p j) c -> p j c", j=2)

    with ExitStack() as ctx:
        keep = ctx.enter_context(tc.tile_pool(name="keep", bufs=1))
        w_stage = ctx.enter_context(tc.tile_pool(name="w_stage", bufs=4))
        x_stage = ctx.enter_context(tc.tile_pool(name="x_stage", bufs=5))
        psum = ctx.enter_context(tc.psum_pool(name="psum", bufs=1))
        ctx.enter_context(tc.manual_schedule())

        identity = keep.tile([P, P], F32, name="identity")
        make_identity(nc, identity[:])

        w_pairs = [keep.tile([P, 2, C], BF16, name="w_raw%d" % i) for i in range(M_TILES // 2)]
        w_raw = [w_pairs[m // 2][:, m % 2, :] for m in range(M_TILES)]
        w_codes = [
            keep.tile([P, PASSES * P], U32, name="w_codes%d" % m, align_bytes=64)
            for m in range(M_TILES)
        ]
        w_scales = [
            keep.tile([P, PASSES * P], U8, name="w_scales%d" % m, align_bytes=64)
            for m in range(M_TILES)
        ]
        x_raw = [
            [keep.tile([P, PACK, N_BLOCK], BF16, name="x_raw%d_%d" % (b, g)) for g in range(PASSES)]
            for b in range(N_BLOCKS)
        ]
        x_codes = [
            [
                keep.tile([P, N_BLOCK], U32, name="x_codes%d_%d" % (b, g), align_bytes=64)
                for g in range(PASSES)
            ]
            for b in range(N_BLOCKS)
        ]
        x_scales = [
            [
                keep.tile([P, N_BLOCK], U8, name="x_scales%d_%d" % (b, g), align_bytes=64)
                for g in range(PASSES)
            ]
            for b in range(N_BLOCKS)
        ]
        w_grouped = {}
        x_grouped = {}
        open_sums = {}
        finished = []

        def load_weight_pair(i):
            nc.sync.dma_start(out=w_pairs[i][:], in_=pair_rows(w_phi, w_g, i))

        def load_weights(m):
            nc.sync.dma_start(out=w_raw[m], in_=pair_rows(w_phi, w_g, m // 2)[:, m % 2, :])

        def load_x(b, g):
            nc.sync.dma_start(
                out=x_raw[b][g][:],
                in_=x_rows[
                    g * K_PASS : (g + 1) * K_PASS, b * N_BLOCK : (b + 1) * N_BLOCK
                ].rearrange("(p t) n -> p t n", t=PACK),
            )

        def shared_bank(i):
            return "bank%d" % (i % BANKS)

        def flip_weights(m):
            grouped = w_stage.tile([P, C], BF16, name="w_grouped", tag="w_grouped", align_bytes=64)
            grouped_words = grouped[:].bitcast(F32).rearrange(
                "p (g o u) -> p g o u", g=PASSES, o=P, u=2
            )
            raw_words = w_raw[m].bitcast(F32)
            passes_in_bank = BANK_BLOCKS // 2
            for bank in range(WORD_BLOCKS // BANK_BLOCKS):
                flipped = psum.tile(
                    [P, BANK_BLOCKS, P], F32, name="flipped",
                    tag=shared_bank(2 * m + bank),
                )
                for q in range(BANK_BLOCKS):
                    g, u = divmod(bank * BANK_BLOCKS + q, 2)
                    nc.tensor.transpose(
                        flipped[:, q, :],
                        raw_words[:, 2 * g * WORDS + u : 2 * (g + 1) * WORDS : 2],
                        identity[:],
                    )
                copy = nc.scalar.copy
                if bank == 1 and m in VECTOR_EMPTIES:
                    copy = nc.vector.tensor_copy
                copy(
                    out=grouped_words[:, bank * passes_in_bank : (bank + 1) * passes_in_bank],
                    in_=flipped[:].rearrange("p (g u) o -> p g o u", u=2),
                )
            w_grouped[m] = grouped

        def quantise_weights(m):
            nc.vector.quantize_mx(
                out=w_codes[m][:].bitcast(FP8X4),
                scales=w_scales[m][:],
                in_=w_grouped[m][:],
            )

        def regrouped(b, g):
            if (b, g) not in x_grouped:
                x_grouped[(b, g)] = x_stage.tile(
                    [P, N_BLOCK, PACK], BF16, name="x_grouped", tag="x_grouped", align_bytes=64
                )
            target = x_grouped[(b, g)][:].rearrange("p (c r) t -> p c t r", r=RUN)
            source = x_raw[b][g][:].rearrange("p t (c r) -> p c t r", r=RUN)
            return target, source

        def vector_runs(b, g):
            return VECTOR_RUNS[b][g]

        def regroup_on_vector(b, g):
            target, source = regrouped(b, g)
            share = slice(0, vector_runs(b, g))
            nc.vector.tensor_copy(out=target[:, share], in_=source[:, share])

        def regroup_on_scalar(b, g):
            target, source = regrouped(b, g)
            share = slice(vector_runs(b, g), RUNS)
            if vector_runs(b, g) < RUNS:
                nc.scalar.copy(out=target[:, share], in_=source[:, share])

        def quantise_x(b, g):
            nc.vector.quantize_mx(
                out=x_codes[b][g][:].bitcast(FP8X4),
                scales=x_scales[b][g][:],
                in_=x_grouped[(b, g)][:].rearrange("p n t -> p (n t)"),
            )

        def multiply(s, g, part=0, parts=1):
            b, m = divmod(s, M_TILES)
            width = N_BLOCK // parts
            pixels = slice(part * width, (part + 1) * width)
            if g == 0:
                open_sums[(s, part)] = psum.tile(
                    [P, width], F32, name="acc", tag=shared_bank(2 * M_TILES + s + part)
                )
            nc.tensor.matmul_mx(
                out=open_sums[(s, part)][:],
                lhsT=w_codes[m][:, g * P : (g + 1) * P].bitcast(FP8X4),
                lhsT_scale=w_scales[m][:, g * P : (g + 1) * P],
                rhs=x_codes[b][g][:, pixels].bitcast(FP8X4),
                rhs_scale=x_scales[b][g][:, pixels],
                start=(g == 0),
                stop=(g == PASSES - 1),
            )
            if g == PASSES - 1:
                finished.append((s, part, parts))

        def pool_tiles(keep_back):
            while len(finished) > keep_back:
                s, part, parts = finished[0]
                finished.remove(finished[0])
                b, m = divmod(s, M_TILES)
                pooled = keep.tile(
                    [P, POOLED_ROWS // parts, POOLED_WIDTH], F32, name="pooled%d_%d" % (s, part)
                )
                nc.vector.tensor_reduce(
                    out=pooled[:],
                    in_=open_sums[(s, part)][:].rearrange(
                        "p (i a j b) -> p i j a b",
                        i=POOLED_ROWS // parts, a=2, j=POOLED_WIDTH, b=2,
                    ),
                    axis=mybir.AxisListType.XY,
                    op=mybir.AluOpType.max,
                )
                width = POOLED_BLOCK // parts
                first = b * POOLED_BLOCK + part * width
                nc.sync.dma_start(
                    out=pair_rows(phi_rows, g_rows, m // 2)[:, m % 2, first : first + width],
                    in_=pooled[:].rearrange("p i j -> p (i j)"),
                )

        def regroup_x(b, g):
            regroup_on_vector(b, g)
            regroup_on_scalar(b, g)

        load_weights(0)
        load_weights(1)
        for i in range(1, EARLY_TILES // 2):
            load_weight_pair(i)
        load_x(0, 0)
        for m in range(EARLY_TILES, M_TILES):
            load_weights(m)
        for b in range(N_BLOCKS):
            for g in range(PASSES):
                if (b, g) != (0, 0):
                    load_x(b, g)

        for m in range(EARLY_TILES):
            flip_weights(m)
            if 0 < m < EARLY_TILES - 1:
                quantise_weights(m - 1)
        regroup_x(0, 0)
        quantise_weights(6)
        flip_weights(8)
        quantise_x(0, 0)
        quantise_weights(7)
        flip_weights(9)
        regroup_x(0, 1)
        quantise_weights(8)
        quantise_x(0, 1)
        quantise_weights(9)

        def whole_tile(s):
            for g in range(PASSES):
                multiply(s, g)

        passes = [(b, g) for b in range(2) for g in range(PASSES)]
        for g in range(PASSES):
            for s in range(FIRST_TILES):
                multiply(s, g)
            if 0 < g < PASSES - 1:
                quantise_x(0, g + 1)
            if g < PASSES - 1:
                regroup_x(*passes[g + 2])

        pool_tiles(FIRST_TILES - 1)
        regroup_x(1, 1)
        pool_tiles(FIRST_TILES - 2)
        quantise_x(1, 0)
        pool_tiles(POOL_LAG + 1)
        whole_tile(FIRST_TILES)
        pool_tiles(POOL_LAG)
        whole_tile(FIRST_TILES + 1)
        regroup_x(1, 2)
        quantise_x(1, 1)
        pool_tiles(POOL_LAG)
        for g in range(PASSES):
            for m in range(SECOND_TILES):
                multiply(M_TILES + m, g)
            if g + 3 < PASSES:
                regroup_x(1, g + 3)
            if g + 2 < PASSES:
                quantise_x(1, g + 2)

        for s in range(M_TILES + SECOND_TILES, TILES - 1):
            b, m = divmod(s, M_TILES)
            left = M_TILES - SECOND_TILES if b == 1 else M_TILES
            for g in range(PASSES):
                beside = M_TILES - left + g * left // PASSES
                if b + 1 < N_BLOCKS and beside == m:
                    regroup_x(b + 1, g)
                if b + 1 < N_BLOCKS and min(beside + 2, M_TILES - 1) == m:
                    quantise_x(b + 1, g)
            pool_tiles(POOL_LAG)
            whole_tile(s)

        for part in range(2):
            pool_tiles(1)
            for g in range(PASSES):
                multiply(TILES - 1, g, part, 2)
        pool_tiles(0)
